import numpy as np
import ml_dtypes


def mxq(x, axis, fmt="e4m3"):
    dtype, down = {"e4m3": (ml_dtypes.float8_e4m3fn, 7), "e5m2": (ml_dtypes.float8_e5m2, 14)}[fmt]
    v = np.moveaxis(np.asarray(x, np.float32).astype(ml_dtypes.bfloat16).astype(np.float64), axis, -1)
    blocks = v.reshape(v.shape[:-1] + (-1, 32))
    amax = np.abs(blocks).max(-1, keepdims=True)
    byte = np.maximum(np.where(amax > 0, np.frexp(amax)[1] - 1 + 127, 0) - down, 1)
    scale = np.exp2(byte - 127.0)
    codes = (blocks / scale).astype(np.float32).astype(dtype).astype(np.float64)
    return np.moveaxis((codes * scale).reshape(v.shape), -1, axis)


WIDE = False


def mx_kscale(k):
    if not WIDE:
        return np.ones(k)
    levels = np.array([10, -10, 5, -5, 0])
    a = np.random.permutation(np.resize(levels, k // 512 * 4)).reshape(k // 512, 4)
    idx = np.arange(k)
    return np.exp2(a[idx // 512, idx % 128 // 32])


BF16 = ml_dtypes.bfloat16


def bf(x):
    return np.asarray(x, np.float32).astype(BF16)


def f64(x):
    return np.asarray(x).astype(np.float64)


E2M1 = np.array([0.0, 0.5, 1.0, 1.5, 2.0, 3.0, 4.0, 6.0, -0.0, -0.5, -1.0, -1.5, -2.0, -3.0, -4.0, -6.0])


def pack_weight(w, fmt):
    k, n = w.shape
    w = f64(bf(w)).reshape(k // 32, 32, n)
    amax = np.abs(w).max(1)
    if fmt == "e4m3":
        byte = np.frexp(amax)[1] - 1 + 127 - 7
    else:
        mant, ex = np.frexp(amax / 6.0)
        byte = np.where(mant > 0.5, ex, ex - 1) + 127
    byte = np.clip(np.where(amax > 0, byte, 1), 1, 254)
    scaled = (w * np.exp2(127.0 - byte)[:, None, :]).reshape(k, n).astype(np.float32)
    by_word = np.ascontiguousarray(scaled.reshape(k // 512, 128, 4, n).transpose(0, 1, 3, 2))
    if fmt == "e4m3":
        words = by_word.astype(ml_dtypes.float8_e4m3fn).view(np.uint8)
    else:
        c = by_word.astype(ml_dtypes.float4_e2m1fn).view(np.uint8) & 0xF
        words = c[..., 0::2] | (c[..., 1::2] << 4)
    return np.ascontiguousarray(words), np.ascontiguousarray(byte.astype(np.uint8).reshape(k // 512, 16, n))


def unpack_weight(words, scales, fmt):
    g, p, n, _ = words.shape
    if fmt == "e4m3":
        vals = np.ascontiguousarray(words).view(ml_dtypes.float8_e4m3fn).astype(np.float64)
    else:
        nib = np.empty((g, p, n, 4), np.uint8)
        nib[..., 0::2] = words & 0xF
        nib[..., 1::2] = words >> 4
        vals = E2M1[nib]
    vals = vals * np.repeat(np.exp2(scales.astype(np.float64) - 127.0), 8, axis=1)[..., None]
    return vals.transpose(0, 1, 3, 2).reshape(g * 512, n)


B, S, I, O, NB, G = 2, 256, 1024, 1024, 5, 1


def setup_inputs():
    s = mx_kscale(I)
    x = bf(np.random.standard_normal((B, S, I)) * s)
    basis_coeffs = bf(np.random.standard_normal((I, O // G, NB)) / np.sqrt(I))
    linear_w = np.random.standard_normal((O, I)) / np.sqrt(I) / s
    linear_w_words, linear_w_scales = pack_weight(np.ascontiguousarray(linear_w.T), "e4m3")
    pathway_balance = bf(0.5 + 0.1 * np.random.standard_normal(2))
    return {"x": x,
            "basis_coeffs": basis_coeffs,
            "linear_w_words": linear_w_words,
            "linear_w_scales": linear_w_scales,
            "pathway_balance": pathway_balance}


def reference(x, basis_coeffs, linear_w_words, linear_w_scales, pathway_balance):
    x = f64(x)
    pathway_balance = f64(pathway_balance)
    shape = x.shape[:-1]
    x_flat = x.reshape(-1, I)
    x_norm = np.tanh(x_flat)
    powers = np.arange(NB, dtype=np.float64)
    basis = x_norm[..., None] ** powers
    bq = mxq(basis, 1, "e4m3").transpose(2, 0, 1)
    cq = mxq(f64(basis_coeffs), 0, "e4m3").transpose(2, 0, 1)
    nonlinear_out = (bq @ cq).sum(0)
    if G > 1:
        nonlinear_out = np.tile(nonlinear_out, (1, G))
    linear_out = mxq(x_flat, 1, "e4m3") @ unpack_weight(linear_w_words, linear_w_scales, "e4m3")
    y = pathway_balance[0] * nonlinear_out + pathway_balance[1] * linear_out
    return y.reshape(*shape, O)

@@ -1,0 +1,216 @@
+from contextlib import ExitStack
+
+import concourse.mybir as mybir
+from concourse.masks import make_identity
+
+F32 = mybir.dt.float32
+BF16 = mybir.dt.bfloat16
+I32 = mybir.dt.int32
+U32 = mybir.dt.uint32
+U8 = mybir.dt.uint8
+FP8X4 = mybir.dt.float8_e4m3fn_x4
+ACT = mybir.ActivationFunctionType
+ALU = mybir.AluOpType
+
+P = 128
+PACK = 4
+K_PASS = P * PACK
+ROWS = 512
+FEATURES = 1024
+OUTS = 1024
+POWERS = 5
+ROW_TILES = ROWS // P
+PASSES = FEATURES // K_PASS
+BANK = 512
+O_CHUNK = 256
+O_CHUNKS = OUTS // O_CHUNK
+WIDTH = O_CHUNK * PACK
+VECTOR_POWERS = 2
+
+FLOPS = 2 * ROWS * OUTS * FEATURES * (POWERS + 1)
+
+
+def tile_kolmogorovarnoldlinear_kernel(
+    tc, x, basis_coeffs, linear_w_words, linear_w_scales, pathway_balance, out
+):
+    nc = tc.nc
+    x_rows = x.flatten_outer_dims().rearrange("(m r) i -> m r i", r=P)
+    out_rows = out.flatten_outer_dims().rearrange("(m r) o -> m r o", r=P)
+    coeff_rows = basis_coeffs.rearrange("(g p j) o n -> g p j (o n)", p=P, j=PACK)
+    w_scale_rows = linear_w_scales.rearrange("g (b r) o -> r b g o", r=4)
+    chunks = [(q, g) for q in range(O_CHUNKS) for g in range(PASSES)]
+
+    with ExitStack() as ctx:
+        ctx.enter_context(tc.manual_schedule())
+        keep = ctx.enter_context(tc.tile_pool(name="keep", bufs=1))
+        raws = ctx.enter_context(tc.tile_pool(name="raws", bufs=len(chunks)))
+        work = ctx.enter_context(tc.tile_pool(name="work", bufs=2))
+        stage = ctx.enter_context(tc.tile_pool(name="stage", bufs=3))
+        psum = ctx.enter_context(tc.psum_pool(name="psum", bufs=8))
+
+        x_sb = []
+        for m in range(ROW_TILES):
+            x_tile = keep.tile([P, FEATURES], BF16, name="x_sb%d" % m)
+            nc.sync.dma_start(out=x_tile[:], in_=x_rows[m])
+            x_sb.append(x_tile)
+
+        w_codes = keep.tile([P, PASSES, OUTS], U32, align_bytes=64)
+        w_scales = keep.tile([P, PASSES, OUTS], U8, align_bytes=64)
+        nc.vector.memset(w_scales[:].bitcast(I32), 0)
+        for r in range(4):
+            nc.sync.dma_start(out=w_scales[r:P:32, :, :].bitcast(I32), in_=w_scale_rows[r].bitcast(I32))
+        for g in range(PASSES):
+            nc.sync.dma_start(
+                out=w_codes[:, g, :].bitcast(I32),
+                in_=linear_w_words[g].rearrange("p o t -> p (o t)").bitcast(I32),
+            )
+
+        raw = {}
+        for q, g in chunks:
+            raw_tile = raws.tile([P, PACK, O_CHUNK * POWERS], BF16, name="raw")
+            nc.sync.dma_start(
+                out=raw_tile[:],
+                in_=coeff_rows[g][:, :, q * O_CHUNK * POWERS : (q + 1) * O_CHUNK * POWERS],
+            )
+            raw[(q, g)] = raw_tile
+
+        balance_bf = keep.tile([P, 2], BF16)
+        nc.scalar.dma_start(out=balance_bf[:], in_=pathway_balance.partition_broadcast(P))
+
+        warm = keep.tile([P, 1], F32)
+        nc.vector.memset(warm[:], 0.0)
+        nc.scalar.activation(out=warm[:], in_=warm[:], func=ACT.Tanh)
+
+        ident = keep.tile([P, P], F32)
+        make_identity(nc, ident[:])
+
+        balance = keep.tile([P, 2], F32)
+        nc.gpsimd.tensor_copy(out=balance[:], in_=balance_bf[:])
+
+        ones_bf = keep.tile([P, P * PACK], BF16, align_bytes=64)
+        ones_codes = keep.tile([P, P], U32, align_bytes=64)
+        ones_scales = keep.tile([P, P], U8, align_bytes=64)
+        nc.vector.memset(ones_bf[:], 1.0)
+        nc.vector.quantize_mx(out=ones_codes[:].bitcast(FP8X4), scales=ones_scales[:], in_=ones_bf[:])
+
+        act_codes = keep.tile([P, ROW_TILES, POWERS, PASSES * P], U32, align_bytes=64)
+        act_scales = keep.tile([P, ROW_TILES, POWERS, PASSES * P], U8, align_bytes=64)
+        y_sb = keep.tile([P, ROW_TILES, OUTS], F32)
+
+        x_t = []
+        for m in range(ROW_TILES):
+            xt_tile = psum.tile([P, 2, PASSES, P], F32, tag="bank", name="x_t%d" % m)
+            x_words = x_sb[m][:].bitcast(F32)
+            for g in range(PASSES):
+                for u in range(2):
+                    nc.tensor.transpose(
+                        xt_tile[:, u, g, :],
+                        x_words[:, g * 2 * P + u : (g + 1) * 2 * P : 2],
+                        ident[:],
+                    )
+            x_t.append(xt_tile)
+
+        for m in range(ROW_TILES):
+            x_grouped = work.tile([P, PASSES * P * PACK], BF16, align_bytes=64)
+            nc.scalar.copy(
+                out=x_grouped[:].bitcast(F32).rearrange("p (s u) -> p s u", u=2),
+                in_=x_t[m][:].rearrange("p u g r -> p (g r) u"),
+            )
+            nc.vector.quantize_mx(
+                out=act_codes[:, m, 0, :].bitcast(FP8X4), scales=act_scales[:, m, 0, :], in_=x_grouped[:]
+            )
+            t1 = work.tile([P, PASSES * P * PACK], F32)
+            nc.scalar.activation(
+                out=t1[:].rearrange("p (s u e) -> p s u e", u=2, e=2),
+                in_=x_t[m][:].bitcast(BF16).rearrange("p u g (r e) -> p (g r) u e", e=2),
+                func=ACT.Tanh,
+            )
+            t2 = work.tile([P, PASSES * P * PACK], F32)
+            powers = work.tile([P, POWERS - 1, PASSES * P * PACK], BF16, align_bytes=64)
+            nc.vector.tensor_copy(out=powers[:, 0, :], in_=t1[:])
+            nc.scalar.activation(out=t2[:], in_=t1[:], func=ACT.Square)
+            nc.vector.tensor_copy(out=powers[:, 1, :], in_=t2[:])
+            nc.vector.tensor_tensor(out=powers[:, 2, :], in0=t2[:], in1=t1[:], op=ALU.mult)
+            nc.scalar.activation(out=powers[:, 3, :], in_=t2[:], func=ACT.Square)
+
+            for h in range(OUTS // BANK):
+                cols = slice(h * BANK, (h + 1) * BANK)
+                l_acc = psum.tile([P, BANK], F32, tag="bank", name="l_acc")
+                for g in range(PASSES):
+                    rows = slice(g * P, (g + 1) * P)
+                    nc.tensor.matmul_mx(
+                        out=l_acc[:],
+                        lhsT=act_codes[:, m, 0, rows].bitcast(FP8X4),
+                        lhsT_scale=act_scales[:, m, 0, rows],
+                        rhs=w_codes[:, g, cols].bitcast(FP8X4),
+                        rhs_scale=w_scales[:, g, cols],
+                        start=(g == 0),
+                        stop=(g == PASSES - 1),
+                    )
+                if h == 0:
+                    nc.scalar.activation(out=y_sb[:, m, cols], in_=l_acc[:], func=ACT.Copy, scale=balance[:, 1:2])
+                else:
+                    nc.vector.tensor_scalar_mul(out=y_sb[:, m, cols], in0=l_acc[:], scalar1=balance[:, 1:2])
+
+            nc.vector.quantize_mx(
+                out=act_codes[:, m, 1:POWERS, :].rearrange("p n c -> p (n c)").bitcast(FP8X4),
+                scales=act_scales[:, m, 1:POWERS, :].rearrange("p n c -> p (n c)"),
+                in_=powers[:].rearrange("p n c -> p (n c)"),
+            )
+
+        def regroup(chunk):
+            src = raw[chunk][:].rearrange("p j (o n) -> p o j n", n=POWERS)
+            by_vector = stage.tile([P, VECTOR_POWERS, WIDTH], BF16, align_bytes=64, name="by_vector")
+            by_scalar = stage.tile([P, POWERS - VECTOR_POWERS, WIDTH], BF16, align_bytes=64, name="by_scalar")
+            nc.vector.tensor_copy(
+                out=by_vector[:].rearrange("p n (o j) -> p o j n", j=PACK), in_=src[:, :, :, 0:VECTOR_POWERS]
+            )
+            nc.scalar.copy(
+                out=by_scalar[:].rearrange("p n (o j) -> p o j n", j=PACK), in_=src[:, :, :, VECTOR_POWERS:POWERS]
+            )
+            return [by_vector[:, n, :] for n in range(VECTOR_POWERS)] + [
+                by_scalar[:, n, :] for n in range(POWERS - VECTOR_POWERS)
+            ]
+
+        def finish(q, n_acc):
+            cols = slice(q * O_CHUNK, (q + 1) * O_CHUNK)
+            for m in range(ROW_TILES):
+                nc.vector.scalar_tensor_tensor(
+                    out=y_sb[:, m, cols],
+                    in0=n_acc[m][:],
+                    scalar=balance[:, 0:1],
+                    in1=y_sb[:, m, cols],
+                    op0=ALU.mult,
+                    op1=ALU.add,
+                )
+                nc.sync.dma_start(out=out_rows[m][:, cols], in_=y_sb[:, m, cols])
+
+        grouped = {chunks[0]: regroup(chunks[0])}
+        n_acc = {}
+        for c, (q, g) in enumerate(chunks):
+            if c + 1 < len(chunks):
+                grouped[chunks[c + 1]] = regroup(chunks[c + 1])
+            c_codes = stage.tile([P, POWERS, O_CHUNK], U32, align_bytes=64)
+            c_scales = stage.tile([P, POWERS, O_CHUNK], U8, align_bytes=64)
+            if g == 0:
+                n_acc[q] = [
+                    psum.tile([P, O_CHUNK], F32, tag="bank", name="n_acc%d" % m) for m in range(ROW_TILES)
+                ]
+            rows = slice(g * P, (g + 1) * P)
+            for n in range(POWERS):
+                nc.vector.quantize_mx(
+                    out=c_codes[:, n, :].bitcast(FP8X4), scales=c_scales[:, n, :], in_=grouped[(q, g)][n]
+                )
+                for m in range(ROW_TILES):
+                    nc.tensor.matmul_mx(
+                        out=n_acc[q][m][:],
+                        lhsT=(ones_codes[:] if n == 0 else act_codes[:, m, n, rows]).bitcast(FP8X4),
+                        lhsT_scale=(ones_scales[:] if n == 0 else act_scales[:, m, n, rows]),
+                        rhs=c_codes[:, n, :].bitcast(FP8X4),
+                        rhs_scale=c_scales[:, n, :],
+                        start=(g == 0 and n == 0),
+                        stop=(g == PASSES - 1 and n == POWERS - 1),
+                    )
+            if g == 0 and q > 0:
+                finish(q - 1, n_acc[q - 1])
+        finish(O_CHUNKS - 1, n_acc[O_CHUNKS - 1])

@@ -74,8 +74,9 @@ def tile_kolmogorovarnoldlinear_kernel(
             )
             raw[(q, g)] = raw_tile
 
-        balance_bf = keep.tile([P, 2], BF16)
-        nc.scalar.dma_start(out=balance_bf[:], in_=pathway_balance.partition_broadcast(P))
+        balance_row = keep.tile([P, 32], BF16)
+        nc.gpsimd.memset(balance_row[:], 0.0)
+        nc.scalar.dma_start(out=balance_row[0:1, 0:2], in_=pathway_balance.unsqueeze(0))
 
         warm = keep.tile([P, 1], F32)
         nc.vector.memset(warm[:], 0.0)
@@ -84,14 +85,16 @@ def tile_kolmogorovarnoldlinear_kernel(
         ident = keep.tile([P, P], F32)
         make_identity(nc, ident[:])
 
-        balance = keep.tile([P, 2], F32)
-        nc.gpsimd.tensor_copy(out=balance[:], in_=balance_bf[:])
-
         ones_bf = keep.tile([P, P * PACK], BF16, align_bytes=64)
         ones_codes = keep.tile([P, P], U32, align_bytes=64)
         ones_scales = keep.tile([P, P], U8, align_bytes=64)
         nc.vector.memset(ones_bf[:], 1.0)
         nc.vector.quantize_mx(out=ones_codes[:].bitcast(FP8X4), scales=ones_scales[:], in_=ones_bf[:])
+
+        balance_ps = psum.tile([P, 32], F32, tag="bank")
+        nc.tensor.matmul(out=balance_ps[:], lhsT=ones_bf[:, 0:P], rhs=balance_row[:], start=True, stop=True)
+        balance = keep.tile([P, 2], F32)
+        nc.vector.tensor_copy(out=balance[:], in_=balance_ps[:, 0:2])
 
         act_codes = keep.tile([P, ROW_TILES, POWERS, PASSES * P], U32, align_bytes=64)
         act_scales = keep.tile([P, ROW_TILES, POWERS, PASSES * P], U8, align_bytes=64)

@@ -91,11 +91,6 @@ def tile_kolmogorovarnoldlinear_kernel(
         nc.vector.memset(ones_bf[:], 1.0)
         nc.vector.quantize_mx(out=ones_codes[:].bitcast(FP8X4), scales=ones_scales[:], in_=ones_bf[:])
 
-        balance_ps = psum.tile([P, 32], F32, tag="bank")
-        nc.tensor.matmul(out=balance_ps[:], lhsT=ones_bf[:, 0:P], rhs=balance_row[:], start=True, stop=True)
-        balance = keep.tile([P, 2], F32)
-        nc.vector.tensor_copy(out=balance[:], in_=balance_ps[:, 0:2])
-
         act_codes = keep.tile([P, ROW_TILES, POWERS, PASSES * P], U32, align_bytes=64)
         act_scales = keep.tile([P, ROW_TILES, POWERS, PASSES * P], U8, align_bytes=64)
         y_sb = keep.tile([P, ROW_TILES, OUTS], F32)
@@ -113,7 +108,9 @@ def tile_kolmogorovarnoldlinear_kernel(
                     )
             x_t.append(xt_tile)
 
-        for m in range(ROW_TILES):
+        t_powers = {}
+
+        def prepare_row_tile(m):
             x_grouped = work.tile([P, PASSES * P * PACK], BF16, align_bytes=64)
             nc.scalar.copy(
                 out=x_grouped[:].bitcast(F32).rearrange("p (s u) -> p s u", u=2),
@@ -135,7 +132,16 @@ def tile_kolmogorovarnoldlinear_kernel(
             nc.vector.tensor_copy(out=powers[:, 1, :], in_=t2[:])
             nc.vector.tensor_tensor(out=powers[:, 2, :], in0=t2[:], in1=t1[:], op=ALU.mult)
             nc.scalar.activation(out=powers[:, 3, :], in_=t2[:], func=ACT.Square)
+            t_powers[m] = powers
 
+        def quantise_powers(m):
+            nc.vector.quantize_mx(
+                out=act_codes[:, m, 1:POWERS, :].rearrange("p n c -> p (n c)").bitcast(FP8X4),
+                scales=act_scales[:, m, 1:POWERS, :].rearrange("p n c -> p (n c)"),
+                in_=t_powers[m][:].rearrange("p n c -> p (n c)"),
+            )
+
+        def linear_part(m):
             for h in range(OUTS // BANK):
                 cols = slice(h * BANK, (h + 1) * BANK)
                 l_acc = psum.tile([P, BANK], F32, tag="bank", name="l_acc")
@@ -155,11 +161,19 @@ def tile_kolmogorovarnoldlinear_kernel(
                 else:
                     nc.vector.tensor_scalar_mul(out=y_sb[:, m, cols], in0=l_acc[:], scalar1=balance[:, 1:2])
 
-            nc.vector.quantize_mx(
-                out=act_codes[:, m, 1:POWERS, :].rearrange("p n c -> p (n c)").bitcast(FP8X4),
-                scales=act_scales[:, m, 1:POWERS, :].rearrange("p n c -> p (n c)"),
-                in_=powers[:].rearrange("p n c -> p (n c)"),
-            )
+        prepare_row_tile(0)
+        quantise_powers(0)
+
+        balance_ps = psum.tile([P, 32], F32, tag="bank")
+        nc.tensor.matmul(out=balance_ps[:], lhsT=ones_bf[:, 0:P], rhs=balance_row[:], start=True, stop=True)
+        balance = keep.tile([P, 2], F32)
+        nc.vector.tensor_copy(out=balance[:], in_=balance_ps[:, 0:2])
+
+        for m in range(1, ROW_TILES):
+            prepare_row_tile(m)
+            linear_part(m - 1)
+            quantise_powers(m)
+        linear_part(ROW_TILES - 1)
 
         def regroup(chunk):
             src = raw[chunk][:].rearrange("p j (o n) -> p o j n", n=POWERS)

@@ -110,29 +110,44 @@ def tile_kolmogorovarnoldlinear_kernel(
 
         t_powers = {}
 
-        def prepare_row_tile(m):
-            x_grouped = work.tile([P, PASSES * P * PACK], BF16, align_bytes=64)
+        x_grouped = {}
+        t1 = {}
+        t2 = {}
+
+        def copy_x(m):
+            x_grouped[m] = work.tile([P, PASSES * P * PACK], BF16, align_bytes=64, name="x_grouped")
             nc.scalar.copy(
-                out=x_grouped[:].bitcast(F32).rearrange("p (s u) -> p s u", u=2),
+                out=x_grouped[m][:].bitcast(F32).rearrange("p (s u) -> p s u", u=2),
                 in_=x_t[m][:].rearrange("p u g r -> p (g r) u"),
             )
+
+        def quantise_x(m):
             nc.vector.quantize_mx(
-                out=act_codes[:, m, 0, :].bitcast(FP8X4), scales=act_scales[:, m, 0, :], in_=x_grouped[:]
+                out=act_codes[:, m, 0, :].bitcast(FP8X4), scales=act_scales[:, m, 0, :], in_=x_grouped[m][:]
             )
-            t1 = work.tile([P, PASSES * P * PACK], F32)
+
+        def tanh_x(m):
+            t1[m] = work.tile([P, PASSES * P * PACK], F32, bufs=3, name="t1")
             nc.scalar.activation(
-                out=t1[:].rearrange("p (s u e) -> p s u e", u=2, e=2),
+                out=t1[m][:].rearrange("p (s u e) -> p s u e", u=2, e=2),
                 in_=x_t[m][:].bitcast(BF16).rearrange("p u g (r e) -> p (g r) u e", e=2),
                 func=ACT.Tanh,
             )
-            t2 = work.tile([P, PASSES * P * PACK], F32)
-            powers = work.tile([P, POWERS - 1, PASSES * P * PACK], BF16, align_bytes=64)
-            nc.vector.tensor_copy(out=powers[:, 0, :], in_=t1[:])
-            nc.scalar.activation(out=t2[:], in_=t1[:], func=ACT.Square)
-            nc.vector.tensor_copy(out=powers[:, 1, :], in_=t2[:])
-            nc.vector.tensor_tensor(out=powers[:, 2, :], in0=t2[:], in1=t1[:], op=ALU.mult)
-            nc.scalar.activation(out=powers[:, 3, :], in_=t2[:], func=ACT.Square)
-            t_powers[m] = powers
+
+        def round_first(m):
+            t_powers[m] = work.tile([P, POWERS - 1, PASSES * P * PACK], BF16, align_bytes=64, name="powers")
+            nc.vector.tensor_copy(out=t_powers[m][:, 0, :], in_=t1[m][:])
+
+        def square(m):
+            t2[m] = work.tile([P, PASSES * P * PACK], F32, name="t2")
+            nc.scalar.activation(out=t2[m][:], in_=t1[m][:], func=ACT.Square)
+
+        def round_second_and_cube(m):
+            nc.vector.tensor_copy(out=t_powers[m][:, 1, :], in_=t2[m][:])
+            nc.vector.tensor_tensor(out=t_powers[m][:, 2, :], in0=t2[m][:], in1=t1[m][:], op=ALU.mult)
+
+        def fourth(m):
+            nc.scalar.activation(out=t_powers[m][:, 3, :], in_=t2[m][:], func=ACT.Square)
 
         def quantise_powers(m):
             nc.vector.quantize_mx(
@@ -161,20 +176,6 @@ def tile_kolmogorovarnoldlinear_kernel(
                 else:
                     nc.vector.tensor_scalar_mul(out=y_sb[:, m, cols], in0=l_acc[:], scalar1=balance[:, 1:2])
 
-        prepare_row_tile(0)
-        quantise_powers(0)
-
-        balance_ps = psum.tile([P, 32], F32, tag="bank")
-        nc.tensor.matmul(out=balance_ps[:], lhsT=ones_bf[:, 0:P], rhs=balance_row[:], start=True, stop=True)
-        balance = keep.tile([P, 2], F32)
-        nc.vector.tensor_copy(out=balance[:], in_=balance_ps[:, 0:2])
-
-        for m in range(1, ROW_TILES):
-            prepare_row_tile(m)
-            linear_part(m - 1)
-            quantise_powers(m)
-        linear_part(ROW_TILES - 1)
-
         def regroup(chunk):
             src = raw[chunk][:].rearrange("p j (o n) -> p o j n", n=POWERS)
             by_vector = stage.tile([P, VECTOR_POWERS, WIDTH], BF16, align_bytes=64, name="by_vector")
@@ -189,6 +190,32 @@ def tile_kolmogorovarnoldlinear_kernel(
                 by_scalar[:, n, :] for n in range(POWERS - VECTOR_POWERS)
             ]
 
+        copy_x(0)
+        quantise_x(0)
+        tanh_x(0)
+        grouped = {}
+        for m in range(ROW_TILES):
+            if m + 1 < ROW_TILES:
+                copy_x(m + 1)
+                quantise_x(m + 1)
+            round_first(m)
+            square(m)
+            if m + 1 < ROW_TILES:
+                tanh_x(m + 1)
+            round_second_and_cube(m)
+            if m > 0:
+                linear_part(m - 1)
+            else:
+                balance_ps = psum.tile([P, 32], F32, tag="bank")
+                nc.tensor.matmul(out=balance_ps[:], lhsT=ones_bf[:, 0:P], rhs=balance_row[:], start=True, stop=True)
+                balance = keep.tile([P, 2], F32)
+                nc.vector.tensor_copy(out=balance[:], in_=balance_ps[:, 0:2])
+            fourth(m)
+            if m + 1 == ROW_TILES:
+                grouped[chunks[0]] = regroup(chunks[0])
+            quantise_powers(m)
+        linear_part(ROW_TILES - 1)
+
         def finish(q, n_acc):
             cols = slice(q * O_CHUNK, (q + 1) * O_CHUNK)
             for m in range(ROW_TILES):
@@ -202,7 +229,6 @@ def tile_kolmogorovarnoldlinear_kernel(
                 )
                 nc.sync.dma_start(out=out_rows[m][:, cols], in_=y_sb[:, m, cols])
 
-        grouped = {chunks[0]: regroup(chunks[0])}
         n_acc = {}
         for c, (q, g) in enumerate(chunks):
             if c + 1 < len(chunks):

@@ -38,6 +38,7 @@ def tile_kolmogorovarnoldlinear_kernel(
     out_rows = out.flatten_outer_dims().rearrange("(m r) o -> m r o", r=P)
     coeff_rows = basis_coeffs.rearrange("(g p j) o n -> g p j (o n)", p=P, j=PACK)
     w_scale_rows = linear_w_scales.rearrange("g (b r) o -> r b g o", r=4)
+    x_parts = [[range(g, g + 1) for g in range(PASSES)]] + [[range(PASSES)]] * (ROW_TILES - 1)
     chunks = [(q, g) for q in range(O_CHUNKS) for g in range(PASSES)]
 
     with ExitStack() as ctx:
@@ -51,7 +52,9 @@ def tile_kolmogorovarnoldlinear_kernel(
         x_sb = []
         for m in range(ROW_TILES):
             x_tile = keep.tile([P, FEATURES], BF16, name="x_sb%d" % m)
-            nc.sync.dma_start(out=x_tile[:], in_=x_rows[m])
+            for part in x_parts[m]:
+                features = slice(part[0] * K_PASS, (part[-1] + 1) * K_PASS)
+                nc.sync.dma_start(out=x_tile[:, features], in_=x_rows[m][:, features])
             x_sb.append(x_tile)
 
         w_codes = keep.tile([P, PASSES, OUTS], U32, align_bytes=64)
@@ -97,16 +100,19 @@ def tile_kolmogorovarnoldlinear_kernel(
 
         x_t = []
         for m in range(ROW_TILES):
-            xt_tile = psum.tile([P, 2, PASSES, P], F32, tag="bank", name="x_t%d" % m)
             x_words = x_sb[m][:].bitcast(F32)
-            for g in range(PASSES):
-                for u in range(2):
-                    nc.tensor.transpose(
-                        xt_tile[:, u, g, :],
-                        x_words[:, g * 2 * P + u : (g + 1) * 2 * P : 2],
-                        ident[:],
-                    )
-            x_t.append(xt_tile)
+            banks = []
+            for part in x_parts[m]:
+                bank = psum.tile([P, 2, len(part), P], F32, tag="bank", name="x_t%d" % m)
+                for g in part:
+                    for u in range(2):
+                        nc.tensor.transpose(
+                            bank[:, u, g - part[0], :],
+                            x_words[:, g * 2 * P + u : (g + 1) * 2 * P : 2],
+                            ident[:],
+                        )
+                banks.append(bank)
+            x_t.append(banks)
 
         t_powers = {}
 
@@ -114,12 +120,16 @@ def tile_kolmogorovarnoldlinear_kernel(
         t1 = {}
         t2 = {}
 
-        def copy_x(m):
+        def columns(part):
+            return slice(part[0] * P * PACK, (part[-1] + 1) * P * PACK)
+
+        def copy_x(m, copy):
             x_grouped[m] = work.tile([P, PASSES * P * PACK], BF16, align_bytes=64, name="x_grouped")
-            nc.scalar.copy(
-                out=x_grouped[m][:].bitcast(F32).rearrange("p (s u) -> p s u", u=2),
-                in_=x_t[m][:].rearrange("p u g r -> p (g r) u"),
-            )
+            for part, bank in zip(x_parts[m], x_t[m]):
+                copy(
+                    out=x_grouped[m][:, columns(part)].bitcast(F32).rearrange("p (s u) -> p s u", u=2),
+                    in_=bank[:].rearrange("p u g r -> p (g r) u"),
+                )
 
         def quantise_x(m):
             nc.vector.quantize_mx(
@@ -128,11 +138,12 @@ def tile_kolmogorovarnoldlinear_kernel(
 
         def tanh_x(m):
             t1[m] = work.tile([P, PASSES * P * PACK], F32, bufs=3, name="t1")
-            nc.scalar.activation(
-                out=t1[m][:].rearrange("p (s u e) -> p s u e", u=2, e=2),
-                in_=x_t[m][:].bitcast(BF16).rearrange("p u g (r e) -> p (g r) u e", e=2),
-                func=ACT.Tanh,
-            )
+            for part, bank in zip(x_parts[m], x_t[m]):
+                nc.scalar.activation(
+                    out=t1[m][:, columns(part)].rearrange("p (s u e) -> p s u e", u=2, e=2),
+                    in_=bank[:].bitcast(BF16).rearrange("p u g (r e) -> p (g r) u e", e=2),
+                    func=ACT.Tanh,
+                )
 
         def round_first(m):
             t_powers[m] = work.tile([P, POWERS - 1, PASSES * P * PACK], BF16, align_bytes=64, name="powers")
@@ -156,14 +167,16 @@ def tile_kolmogorovarnoldlinear_kernel(
                 in_=t_powers[m][:].rearrange("p n c -> p (n c)"),
             )
 
-        def linear_part(m):
+        l_acc = {}
+
+        def multiply_linear(m):
             for h in range(OUTS // BANK):
                 cols = slice(h * BANK, (h + 1) * BANK)
-                l_acc = psum.tile([P, BANK], F32, tag="bank", name="l_acc")
+                l_acc[m, h] = psum.tile([P, BANK], F32, tag="bank", name="l_acc")
                 for g in range(PASSES):
                     rows = slice(g * P, (g + 1) * P)
                     nc.tensor.matmul_mx(
-                        out=l_acc[:],
+                        out=l_acc[m, h][:],
                         lhsT=act_codes[:, m, 0, rows].bitcast(FP8X4),
                         lhsT_scale=act_scales[:, m, 0, rows],
                         rhs=w_codes[:, g, cols].bitcast(FP8X4),
@@ -171,57 +184,57 @@ def tile_kolmogorovarnoldlinear_kernel(
                         start=(g == 0),
                         stop=(g == PASSES - 1),
                     )
-                if h == 0:
-                    nc.scalar.activation(out=y_sb[:, m, cols], in_=l_acc[:], func=ACT.Copy, scale=balance[:, 1:2])
-                else:
-                    nc.vector.tensor_scalar_mul(out=y_sb[:, m, cols], in0=l_acc[:], scalar1=balance[:, 1:2])
 
-        def regroup(chunk):
-            src = raw[chunk][:].rearrange("p j (o n) -> p o j n", n=POWERS)
-            by_vector = stage.tile([P, VECTOR_POWERS, WIDTH], BF16, align_bytes=64, name="by_vector")
-            by_scalar = stage.tile([P, POWERS - VECTOR_POWERS, WIDTH], BF16, align_bytes=64, name="by_scalar")
-            nc.vector.tensor_copy(
-                out=by_vector[:].rearrange("p n (o j) -> p o j n", j=PACK), in_=src[:, :, :, 0:VECTOR_POWERS]
-            )
-            nc.scalar.copy(
-                out=by_scalar[:].rearrange("p n (o j) -> p o j n", j=PACK), in_=src[:, :, :, VECTOR_POWERS:POWERS]
-            )
-            return [by_vector[:, n, :] for n in range(VECTOR_POWERS)] + [
-                by_scalar[:, n, :] for n in range(POWERS - VECTOR_POWERS)
-            ]
+        def weigh_linear(m):
+            nc.scalar.activation(out=y_sb[:, m, 0:BANK], in_=l_acc[m, 0][:], func=ACT.Copy, scale=balance[:, 1:2])
+            nc.vector.tensor_scalar_mul(out=y_sb[:, m, BANK:OUTS], in0=l_acc[m, 1][:], scalar1=balance[:, 1:2])
 
-        copy_x(0)
-        quantise_x(0)
-        tanh_x(0)
         grouped = {}
-        for m in range(ROW_TILES):
-            if m + 1 < ROW_TILES:
-                copy_x(m + 1)
-                quantise_x(m + 1)
-            round_first(m)
-            square(m)
-            if m + 1 < ROW_TILES:
-                tanh_x(m + 1)
-            round_second_and_cube(m)
-            if m > 0:
-                linear_part(m - 1)
-            else:
-                balance_ps = psum.tile([P, 32], F32, tag="bank")
-                nc.tensor.matmul(out=balance_ps[:], lhsT=ones_bf[:, 0:P], rhs=balance_row[:], start=True, stop=True)
-                balance = keep.tile([P, 2], F32)
-                nc.vector.tensor_copy(out=balance[:], in_=balance_ps[:, 0:2])
-            fourth(m)
-            if m + 1 == ROW_TILES:
-                grouped[chunks[0]] = regroup(chunks[0])
-            quantise_powers(m)
-        linear_part(ROW_TILES - 1)
 
-        def finish(q, n_acc):
+        def regroup(chunk, by_vector, by_scalar):
+            src = raw[chunk][:].rearrange("p j (o n) -> p o j n", n=POWERS)
+            if by_vector:
+                grouped[chunk] = stage.tile([P, POWERS, WIDTH], BF16, align_bytes=64, name="grouped")
+            dst = grouped[chunk][:].rearrange("p n (o j) -> p o j n", j=PACK)
+            if by_vector:
+                nc.vector.tensor_copy(out=dst[:, :, :, 0:VECTOR_POWERS], in_=src[:, :, :, 0:VECTOR_POWERS])
+            if by_scalar:
+                nc.scalar.copy(out=dst[:, :, :, VECTOR_POWERS:POWERS], in_=src[:, :, :, VECTOR_POWERS:POWERS])
+
+        codes = {}
+        scales = {}
+        n_acc = {}
+
+        def quantise(chunk, n):
+            if n == 0:
+                codes[chunk] = stage.tile([P, POWERS, O_CHUNK], U32, align_bytes=64, name="c_codes")
+                scales[chunk] = stage.tile([P, POWERS, O_CHUNK], U8, align_bytes=64, name="c_scales")
+            nc.vector.quantize_mx(
+                out=codes[chunk][:, n, :].bitcast(FP8X4), scales=scales[chunk][:, n, :], in_=grouped[chunk][:, n, :]
+            )
+
+        def multiply(chunk, n, m):
+            q, g = chunk
+            rows = slice(g * P, (g + 1) * P)
+            nc.tensor.matmul_mx(
+                out=n_acc[q][m][:],
+                lhsT=(ones_codes[:] if n == 0 else act_codes[:, m, n, rows]).bitcast(FP8X4),
+                lhsT_scale=(ones_scales[:] if n == 0 else act_scales[:, m, n, rows]),
+                rhs=codes[chunk][:, n, :].bitcast(FP8X4),
+                rhs_scale=scales[chunk][:, n, :],
+                start=(g == 0 and n == 0),
+                stop=(g == PASSES - 1 and n == POWERS - 1),
+            )
+
+        def open_sums(q):
+            n_acc[q] = [psum.tile([P, O_CHUNK], F32, tag="bank", name="n_acc%d" % m) for m in range(ROW_TILES)]
+
+        def finish(q):
             cols = slice(q * O_CHUNK, (q + 1) * O_CHUNK)
             for m in range(ROW_TILES):
                 nc.vector.scalar_tensor_tensor(
                     out=y_sb[:, m, cols],
-                    in0=n_acc[m][:],
+                    in0=n_acc[q][m][:],
                     scalar=balance[:, 0:1],
                     in1=y_sb[:, m, cols],
                     op0=ALU.mult,
@@ -229,31 +242,61 @@ def tile_kolmogorovarnoldlinear_kernel(
                 )
                 nc.sync.dma_start(out=out_rows[m][:, cols], in_=y_sb[:, m, cols])
 
-        n_acc = {}
-        for c, (q, g) in enumerate(chunks):
+        copy_x(0, nc.scalar.copy)
+        quantise_x(0)
+        tanh_x(0)
+        balance_ps = psum.tile([P, 32], F32, tag="bank")
+        nc.tensor.matmul(out=balance_ps[:], lhsT=ones_bf[:, 0:P], rhs=balance_row[:], start=True, stop=True)
+        balance = keep.tile([P, 2], F32)
+        multiply_linear(0)
+        for m in range(ROW_TILES):
+            if m + 1 < ROW_TILES:
+                copy_x(m + 1, nc.vector.tensor_copy if m == 0 else nc.scalar.copy)
+                quantise_x(m + 1)
+                multiply_linear(m + 1)
+                round_first(m)
+            square(m)
+            if m + 1 < ROW_TILES:
+                tanh_x(m + 1)
+            round_second_and_cube(m)
+            if m == 0:
+                nc.vector.tensor_copy(out=balance[:], in_=balance_ps[:, 0:2])
+            else:
+                weigh_linear(m - 1)
+            fourth(m)
+            if m == 2:
+                regroup(chunks[0], True, True)
+            if m == 3:
+                regroup(chunks[1], False, True)
+            quantise_powers(m)
+            if m == 2:
+                round_first(3)
+                regroup(chunks[1], True, False)
+                open_sums(0)
+                for n in range(POWERS):
+                    quantise(chunks[0], n)
+                    for ready in range(3):
+                        multiply(chunks[0], n, ready)
+            if m == 3:
+                for n in range(POWERS):
+                    multiply(chunks[0], n, 3)
+        weigh_linear(ROW_TILES - 1)
+
+        for c in range(1, len(chunks)):
+            q, g = chunks[c]
             if c + 1 < len(chunks):
-                grouped[chunks[c + 1]] = regroup(chunks[c + 1])
-            c_codes = stage.tile([P, POWERS, O_CHUNK], U32, align_bytes=64)
-            c_scales = stage.tile([P, POWERS, O_CHUNK], U8, align_bytes=64)
+                regroup(chunks[c + 1], True, True)
             if g == 0:
-                n_acc[q] = [
-                    psum.tile([P, O_CHUNK], F32, tag="bank", name="n_acc%d" % m) for m in range(ROW_TILES)
-                ]
-            rows = slice(g * P, (g + 1) * P)
+                open_sums(q)
+            whole = POWERS if c + 1 < len(chunks) else POWERS - 2
             for n in range(POWERS):
-                nc.vector.quantize_mx(
-                    out=c_codes[:, n, :].bitcast(FP8X4), scales=c_scales[:, n, :], in_=grouped[(q, g)][n]
-                )
-                for m in range(ROW_TILES):
-                    nc.tensor.matmul_mx(
-                        out=n_acc[q][m][:],
-                        lhsT=(ones_codes[:] if n == 0 else act_codes[:, m, n, rows]).bitcast(FP8X4),
-                        lhsT_scale=(ones_scales[:] if n == 0 else act_scales[:, m, n, rows]),
-                        rhs=c_codes[:, n, :].bitcast(FP8X4),
-                        rhs_scale=c_scales[:, n, :],
-                        start=(g == 0 and n == 0),
-                        stop=(g == PASSES - 1 and n == POWERS - 1),
-                    )
-            if g == 0 and q > 0:
-                finish(q - 1, n_acc[q - 1])
-        finish(O_CHUNKS - 1, n_acc[O_CHUNKS - 1])
+                quantise(chunks[c], n)
+                if n < whole:
+                    for m in range(ROW_TILES):
+                        multiply(chunks[c], n, m)
+            for m in range(ROW_TILES):
+                for n in range(whole, POWERS):
+                    multiply(chunks[c], n, m)
+            if g == 0:
+                finish(q - 1)
+        finish(O_CHUNKS - 1)

@@ -25,6 +25,7 @@ BANK = 512
 O_CHUNK = 256
 O_CHUNKS = OUTS // O_CHUNK
 WIDTH = O_CHUNK * PACK
+PAIR = 2
 VECTOR_POWERS = 2
 
 FLOPS = 2 * ROWS * OUTS * FEATURES * (POWERS + 1)
@@ -192,14 +193,14 @@ def tile_kolmogorovarnoldlinear_kernel(
         grouped = {}
 
         def regroup(chunk, by_vector, by_scalar):
-            src = raw[chunk][:].rearrange("p j (o n) -> p o j n", n=POWERS)
+            src = raw[chunk][:].rearrange("p j (c i n) -> p c j i n", i=PAIR, n=POWERS)
             if by_vector:
                 grouped[chunk] = stage.tile([P, POWERS, WIDTH], BF16, align_bytes=64, name="grouped")
-            dst = grouped[chunk][:].rearrange("p n (o j) -> p o j n", j=PACK)
+            dst = grouped[chunk][:].rearrange("p n (c i j) -> p c j i n", i=PAIR, j=PACK)
             if by_vector:
-                nc.vector.tensor_copy(out=dst[:, :, :, 0:VECTOR_POWERS], in_=src[:, :, :, 0:VECTOR_POWERS])
+                nc.vector.tensor_copy(out=dst[:, :, :, :, 0:VECTOR_POWERS], in_=src[:, :, :, :, 0:VECTOR_POWERS])
             if by_scalar:
-                nc.scalar.copy(out=dst[:, :, :, VECTOR_POWERS:POWERS], in_=src[:, :, :, VECTOR_POWERS:POWERS])
+                nc.scalar.copy(out=dst[:, :, :, :, VECTOR_POWERS:POWERS], in_=src[:, :, :, :, VECTOR_POWERS:POWERS])
 
         codes = {}
         scales = {}
@@ -225,6 +226,12 @@ def tile_kolmogorovarnoldlinear_kernel(
                 start=(g == 0 and n == 0),
                 stop=(g == PASSES - 1 and n == POWERS - 1),
             )
+
+        def quantise_and_multiply(chunk, powers, row_tiles):
+            for n in powers:
+                quantise(chunk, n)
+                for m in row_tiles:
+                    multiply(chunk, n, m)
 
         def open_sums(q):
             n_acc[q] = [psum.tile([P, O_CHUNK], F32, tag="bank", name="n_acc%d" % m) for m in range(ROW_TILES)]
@@ -273,30 +280,29 @@ def tile_kolmogorovarnoldlinear_kernel(
                 round_first(3)
                 regroup(chunks[1], True, False)
                 open_sums(0)
-                for n in range(POWERS):
-                    quantise(chunks[0], n)
-                    for ready in range(3):
-                        multiply(chunks[0], n, ready)
+                quantise_and_multiply(chunks[0], range(POWERS), range(3))
             if m == 3:
                 for n in range(POWERS):
                     multiply(chunks[0], n, 3)
+                quantise_and_multiply(chunks[1], range(VECTOR_POWERS), range(ROW_TILES))
         weigh_linear(ROW_TILES - 1)
 
         for c in range(1, len(chunks)):
             q, g = chunks[c]
-            if c + 1 < len(chunks):
+            last = c + 1 == len(chunks)
+            if not last:
                 regroup(chunks[c + 1], True, True)
-            if g == 0:
-                open_sums(q)
-            whole = POWERS if c + 1 < len(chunks) else POWERS - 2
-            for n in range(POWERS):
+            whole = POWERS - 2 if last else POWERS
+            quantise_and_multiply(chunks[c], range(VECTOR_POWERS, whole), range(ROW_TILES))
+            for n in range(whole, POWERS):
                 quantise(chunks[c], n)
-                if n < whole:
-                    for m in range(ROW_TILES):
-                        multiply(chunks[c], n, m)
             for m in range(ROW_TILES):
                 for n in range(whole, POWERS):
                     multiply(chunks[c], n, m)
+            if not last:
+                if g == PASSES - 1:
+                    open_sums(q + 1)
+                quantise_and_multiply(chunks[c + 1], range(VECTOR_POWERS), range(ROW_TILES))
             if g == 0:
                 finish(q - 1)
         finish(O_CHUNKS - 1)

@@ -200,7 +200,9 @@ def tile_kolmogorovarnoldlinear_kernel(
             if by_vector:
                 nc.vector.tensor_copy(out=dst[:, :, :, :, 0:VECTOR_POWERS], in_=src[:, :, :, :, 0:VECTOR_POWERS])
             if by_scalar:
-                nc.scalar.copy(out=dst[:, :, :, :, VECTOR_POWERS:POWERS], in_=src[:, :, :, :, VECTOR_POWERS:POWERS])
+                ends = (VECTOR_POWERS, POWERS) if chunk != chunks[-1] else (VECTOR_POWERS, POWERS - 1, POWERS)
+                for first, end in zip(ends, ends[1:]):
+                    nc.scalar.copy(out=dst[:, :, :, :, first:end], in_=src[:, :, :, :, first:end])
 
         codes = {}
         scales = {}

from contextlib import ExitStack

import concourse.mybir as mybir
from concourse.masks import make_identity

F32 = mybir.dt.float32
BF16 = mybir.dt.bfloat16
I32 = mybir.dt.int32
U32 = mybir.dt.uint32
U8 = mybir.dt.uint8
FP8X4 = mybir.dt.float8_e4m3fn_x4
ACT = mybir.ActivationFunctionType
ALU = mybir.AluOpType

P = 128
PACK = 4
K_PASS = P * PACK
ROWS = 512
FEATURES = 1024
OUTS = 1024
POWERS = 5
ROW_TILES = ROWS // P
PASSES = FEATURES // K_PASS
BANK = 512
O_CHUNK = 256
O_CHUNKS = OUTS // O_CHUNK
WIDTH = O_CHUNK * PACK
PAIR = 2
VECTOR_POWERS = 2

FLOPS = 2 * ROWS * OUTS * FEATURES * (POWERS + 1)


def tile_kolmogorovarnoldlinear_kernel(
    tc, x, basis_coeffs, linear_w_words, linear_w_scales, pathway_balance, out
):
    nc = tc.nc
    x_rows = x.flatten_outer_dims().rearrange("(m r) i -> m r i", r=P)
    out_rows = out.flatten_outer_dims().rearrange("(m r) o -> m r o", r=P)
    coeff_rows = basis_coeffs.rearrange("(g p j) o n -> g p j (o n)", p=P, j=PACK)
    w_scale_rows = linear_w_scales.rearrange("g (b r) o -> r b g o", r=4)
    x_parts = [[range(g, g + 1) for g in range(PASSES)]] + [[range(PASSES)]] * (ROW_TILES - 1)
    chunks = [(q, g) for q in range(O_CHUNKS) for g in range(PASSES)]

    with ExitStack() as ctx:
        ctx.enter_context(tc.manual_schedule())
        keep = ctx.enter_context(tc.tile_pool(name="keep", bufs=1))
        raws = ctx.enter_context(tc.tile_pool(name="raws", bufs=len(chunks)))
        work = ctx.enter_context(tc.tile_pool(name="work", bufs=2))
        stage = ctx.enter_context(tc.tile_pool(name="stage", bufs=3))
        psum = ctx.enter_context(tc.psum_pool(name="psum", bufs=8))

        x_sb = []
        for m in range(ROW_TILES):
            x_tile = keep.tile([P, FEATURES], BF16, name="x_sb%d" % m)
            for part in x_parts[m]:
                features = slice(part[0] * K_PASS, (part[-1] + 1) * K_PASS)
                nc.sync.dma_start(out=x_tile[:, features], in_=x_rows[m][:, features])
            x_sb.append(x_tile)

        w_codes = keep.tile([P, PASSES, OUTS], U32, align_bytes=64)
        w_scales = keep.tile([P, PASSES, OUTS], U8, align_bytes=64)
        nc.vector.memset(w_scales[:].bitcast(I32), 0)
        for r in range(4):
            nc.sync.dma_start(out=w_scales[r:P:32, :, :].bitcast(I32), in_=w_scale_rows[r].bitcast(I32))
        for g in range(PASSES):
            nc.sync.dma_start(
                out=w_codes[:, g, :].bitcast(I32),
                in_=linear_w_words[g].rearrange("p o t -> p (o t)").bitcast(I32),
            )

        raw = {}
        for q, g in chunks:
            raw_tile = raws.tile([P, PACK, O_CHUNK * POWERS], BF16, name="raw")
            nc.sync.dma_start(
                out=raw_tile[:],
                in_=coeff_rows[g][:, :, q * O_CHUNK * POWERS : (q + 1) * O_CHUNK * POWERS],
            )
            raw[(q, g)] = raw_tile

        balance_row = keep.tile([P, 32], BF16)
        nc.gpsimd.memset(balance_row[:], 0.0)
        nc.scalar.dma_start(out=balance_row[0:1, 0:2], in_=pathway_balance.unsqueeze(0))

        warm = keep.tile([P, 1], F32)
        nc.vector.memset(warm[:], 0.0)
        nc.scalar.activation(out=warm[:], in_=warm[:], func=ACT.Tanh)

        ident = keep.tile([P, P], F32)
        make_identity(nc, ident[:])

        ones_bf = keep.tile([P, P * PACK], BF16, align_bytes=64)
        ones_codes = keep.tile([P, P], U32, align_bytes=64)
        ones_scales = keep.tile([P, P], U8, align_bytes=64)
        nc.vector.memset(ones_bf[:], 1.0)
        nc.vector.quantize_mx(out=ones_codes[:].bitcast(FP8X4), scales=ones_scales[:], in_=ones_bf[:])

        act_codes = keep.tile([P, ROW_TILES, POWERS, PASSES * P], U32, align_bytes=64)
        act_scales = keep.tile([P, ROW_TILES, POWERS, PASSES * P], U8, align_bytes=64)
        y_sb = keep.tile([P, ROW_TILES, OUTS], F32)

        x_t = []
        for m in range(ROW_TILES):
            x_words = x_sb[m][:].bitcast(F32)
            banks = []
            for part in x_parts[m]:
                bank = psum.tile([P, 2, len(part), P], F32, tag="bank", name="x_t%d" % m)
                for g in part:
                    for u in range(2):
                        nc.tensor.transpose(
                            bank[:, u, g - part[0], :],
                            x_words[:, g * 2 * P + u : (g + 1) * 2 * P : 2],
                            ident[:],
                        )
                banks.append(bank)
            x_t.append(banks)

        t_powers = {}

        x_grouped = {}
        t1 = {}
        t2 = {}

        def columns(part):
            return slice(part[0] * P * PACK, (part[-1] + 1) * P * PACK)

        def copy_x(m, copy):
            x_grouped[m] = work.tile([P, PASSES * P * PACK], BF16, align_bytes=64, name="x_grouped")
            for part, bank in zip(x_parts[m], x_t[m]):
                copy(
                    out=x_grouped[m][:, columns(part)].bitcast(F32).rearrange("p (s u) -> p s u", u=2),
                    in_=bank[:].rearrange("p u g r -> p (g r) u"),
                )

        def quantise_x(m):
            nc.vector.quantize_mx(
                out=act_codes[:, m, 0, :].bitcast(FP8X4), scales=act_scales[:, m, 0, :], in_=x_grouped[m][:]
            )

        def tanh_x(m):
            t1[m] = work.tile([P, PASSES * P * PACK], F32, bufs=3, name="t1")
            for part, bank in zip(x_parts[m], x_t[m]):
                nc.scalar.activation(
                    out=t1[m][:, columns(part)].rearrange("p (s u e) -> p s u e", u=2, e=2),
                    in_=bank[:].bitcast(BF16).rearrange("p u g (r e) -> p (g r) u e", e=2),
                    func=ACT.Tanh,
                )

        def round_first(m):
            t_powers[m] = work.tile([P, POWERS - 1, PASSES * P * PACK], BF16, align_bytes=64, name="powers")
            nc.vector.tensor_copy(out=t_powers[m][:, 0, :], in_=t1[m][:])

        def square(m):
            t2[m] = work.tile([P, PASSES * P * PACK], F32, name="t2")
            nc.scalar.activation(out=t2[m][:], in_=t1[m][:], func=ACT.Square)

        def round_second_and_cube(m):
            nc.vector.tensor_copy(out=t_powers[m][:, 1, :], in_=t2[m][:])
            nc.vector.tensor_tensor(out=t_powers[m][:, 2, :], in0=t2[m][:], in1=t1[m][:], op=ALU.mult)

        def fourth(m):
            nc.scalar.activation(out=t_powers[m][:, 3, :], in_=t2[m][:], func=ACT.Square)

        def quantise_powers(m):
            nc.vector.quantize_mx(
                out=act_codes[:, m, 1:POWERS, :].rearrange("p n c -> p (n c)").bitcast(FP8X4),
                scales=act_scales[:, m, 1:POWERS, :].rearrange("p n c -> p (n c)"),
                in_=t_powers[m][:].rearrange("p n c -> p (n c)"),
            )

        l_acc = {}

        def multiply_linear(m):
            for h in range(OUTS // BANK):
                cols = slice(h * BANK, (h + 1) * BANK)
                l_acc[m, h] = psum.tile([P, BANK], F32, tag="bank", name="l_acc")
                for g in range(PASSES):
                    rows = slice(g * P, (g + 1) * P)
                    nc.tensor.matmul_mx(
                        out=l_acc[m, h][:],
                        lhsT=act_codes[:, m, 0, rows].bitcast(FP8X4),
                        lhsT_scale=act_scales[:, m, 0, rows],
                        rhs=w_codes[:, g, cols].bitcast(FP8X4),
                        rhs_scale=w_scales[:, g, cols],
                        start=(g == 0),
                        stop=(g == PASSES - 1),
                    )

        def weigh_linear(m):
            nc.scalar.activation(out=y_sb[:, m, 0:BANK], in_=l_acc[m, 0][:], func=ACT.Copy, scale=balance[:, 1:2])
            nc.vector.tensor_scalar_mul(out=y_sb[:, m, BANK:OUTS], in0=l_acc[m, 1][:], scalar1=balance[:, 1:2])

        grouped = {}

        def regroup(chunk, by_vector, by_scalar):
            src = raw[chunk][:].rearrange("p j (c i n) -> p c j i n", i=PAIR, n=POWERS)
            if by_vector:
                grouped[chunk] = stage.tile([P, POWERS, WIDTH], BF16, align_bytes=64, name="grouped")
            dst = grouped[chunk][:].rearrange("p n (c i j) -> p c j i n", i=PAIR, j=PACK)
            if by_vector:
                nc.vector.tensor_copy(out=dst[:, :, :, :, 0:VECTOR_POWERS], in_=src[:, :, :, :, 0:VECTOR_POWERS])
            if by_scalar:
                ends = (VECTOR_POWERS, POWERS) if chunk != chunks[-1] else (VECTOR_POWERS, POWERS - 1, POWERS)
                for first, end in zip(ends, ends[1:]):
                    nc.scalar.copy(out=dst[:, :, :, :, first:end], in_=src[:, :, :, :, first:end])

        codes = {}
        scales = {}
        n_acc = {}

        def quantise(chunk, n):
            if n == 0:
                codes[chunk] = stage.tile([P, POWERS, O_CHUNK], U32, align_bytes=64, name="c_codes")
                scales[chunk] = stage.tile([P, POWERS, O_CHUNK], U8, align_bytes=64, name="c_scales")
            nc.vector.quantize_mx(
                out=codes[chunk][:, n, :].bitcast(FP8X4), scales=scales[chunk][:, n, :], in_=grouped[chunk][:, n, :]
            )

        def multiply(chunk, n, m):
            q, g = chunk
            rows = slice(g * P, (g + 1) * P)
            nc.tensor.matmul_mx(
                out=n_acc[q][m][:],
                lhsT=(ones_codes[:] if n == 0 else act_codes[:, m, n, rows]).bitcast(FP8X4),
                lhsT_scale=(ones_scales[:] if n == 0 else act_scales[:, m, n, rows]),
                rhs=codes[chunk][:, n, :].bitcast(FP8X4),
                rhs_scale=scales[chunk][:, n, :],
                start=(g == 0 and n == 0),
                stop=(g == PASSES - 1 and n == POWERS - 1),
            )

        def quantise_and_multiply(chunk, powers, row_tiles):
            for n in powers:
                quantise(chunk, n)
                for m in row_tiles:
                    multiply(chunk, n, m)

        def open_sums(q):
            n_acc[q] = [psum.tile([P, O_CHUNK], F32, tag="bank", name="n_acc%d" % m) for m in range(ROW_TILES)]

        def finish(q):
            cols = slice(q * O_CHUNK, (q + 1) * O_CHUNK)
            for m in range(ROW_TILES):
                nc.vector.scalar_tensor_tensor(
                    out=y_sb[:, m, cols],
                    in0=n_acc[q][m][:],
                    scalar=balance[:, 0:1],
                    in1=y_sb[:, m, cols],
                    op0=ALU.mult,
                    op1=ALU.add,
                )
                nc.sync.dma_start(out=out_rows[m][:, cols], in_=y_sb[:, m, cols])

        copy_x(0, nc.scalar.copy)
        quantise_x(0)
        tanh_x(0)
        balance_ps = psum.tile([P, 32], F32, tag="bank")
        nc.tensor.matmul(out=balance_ps[:], lhsT=ones_bf[:, 0:P], rhs=balance_row[:], start=True, stop=True)
        balance = keep.tile([P, 2], F32)
        multiply_linear(0)
        for m in range(ROW_TILES):
            if m + 1 < ROW_TILES:
                copy_x(m + 1, nc.vector.tensor_copy if m == 0 else nc.scalar.copy)
                quantise_x(m + 1)
                multiply_linear(m + 1)
                round_first(m)
            square(m)
            if m + 1 < ROW_TILES:
                tanh_x(m + 1)
            round_second_and_cube(m)
            if m == 0:
                nc.vector.tensor_copy(out=balance[:], in_=balance_ps[:, 0:2])
            else:
                weigh_linear(m - 1)
            fourth(m)
            if m == 2:
                regroup(chunks[0], True, True)
            if m == 3:
                regroup(chunks[1], False, True)
            quantise_powers(m)
            if m == 2:
                round_first(3)
                regroup(chunks[1], True, False)
                open_sums(0)
                quantise_and_multiply(chunks[0], range(POWERS), range(3))
            if m == 3:
                for n in range(POWERS):
                    multiply(chunks[0], n, 3)
                quantise_and_multiply(chunks[1], range(VECTOR_POWERS), range(ROW_TILES))
        weigh_linear(ROW_TILES - 1)

        for c in range(1, len(chunks)):
            q, g = chunks[c]
            last = c + 1 == len(chunks)
            if not last:
                regroup(chunks[c + 1], True, True)
            whole = POWERS - 2 if last else POWERS
            quantise_and_multiply(chunks[c], range(VECTOR_POWERS, whole), range(ROW_TILES))
            for n in range(whole, POWERS):
                quantise(chunks[c], n)
            for m in range(ROW_TILES):
                for n in range(whole, POWERS):
                    multiply(chunks[c], n, m)
            if not last:
                if g == PASSES - 1:
                    open_sums(q + 1)
                quantise_and_multiply(chunks[c + 1], range(VECTOR_POWERS), range(ROW_TILES))
            if g == 0:
                finish(q - 1)
        finish(O_CHUNKS - 1)
